import numpy as np
import ml_dtypes


def mxq(x, axis, fmt="e4m3"):
    dtype, down = {"e4m3": (ml_dtypes.float8_e4m3fn, 7), "e5m2": (ml_dtypes.float8_e5m2, 14)}[fmt]
    v = np.moveaxis(np.asarray(x, np.float32).astype(ml_dtypes.bfloat16).astype(np.float64), axis, -1)
    blocks = v.reshape(v.shape[:-1] + (-1, 32))
    amax = np.abs(blocks).max(-1, keepdims=True)
    byte = np.maximum(np.where(amax > 0, np.frexp(amax)[1] - 1 + 127, 0) - down, 1)
    scale = np.exp2(byte - 127.0)
    codes = (blocks / scale).astype(np.float32).astype(dtype).astype(np.float64)
    return np.moveaxis((codes * scale).reshape(v.shape), -1, axis)


WIDE = False


def mx_kscale(k):
    if not WIDE:
        return np.ones(k)
    levels = np.array([10, -10, 5, -5, 0])
    a = np.random.permutation(np.resize(levels, k // 512 * 4)).reshape(k // 512, 4)
    idx = np.arange(k)
    return np.exp2(a[idx // 512, idx % 128 // 32])


BF16 = ml_dtypes.bfloat16


def bf(x):
    return np.asarray(x, np.float32).astype(BF16)


def f64(x):
    return np.asarray(x).astype(np.float64)


B, T, D, E, F = 4, 256, 1024, 1024, 4096
EPS = 1e-6


def rms_norm(x, w):
    rms = np.sqrt(np.mean(x * x, axis=-1, keepdims=True) + EPS)
    return x / rms * w


def erf(v):
    a = np.minimum(np.abs(v), 6.0)
    z = 2.0 * a * a
    term = a.copy()
    tot = a.copy()
    for n in range(1, 110):
        term = term * z / (2 * n + 1)
        tot = tot + term
    return np.sign(v) * tot * np.exp(-a * a) * 2.0 / np.sqrt(np.pi)


def gelu_erf(v):
    return 0.5 * v * (1.0 + erf(v / np.sqrt(2.0)))


def setup_inputs():
    s, t = mx_kscale(E), mx_kscale(D)
    return {"attn": bf(np.random.standard_normal((B, T, E)) * 0.6 * s),
            "x": bf(np.random.standard_normal((B, T, D))),
            "wo": bf(np.random.standard_normal((E, D)) / np.sqrt(E) / s[:, None]),
            "bo": bf(np.random.standard_normal(D) * 0.1),
            "mlp_norm_w": bf((1.0 + 0.1 * np.random.standard_normal(D)) * t),
            "w1": bf(np.random.standard_normal((D, F)) / np.sqrt(D) / t[:, None]),
            "b1": bf(np.random.standard_normal(F) * 0.1)}


def reference(attn, x, wo, bo, mlp_norm_w, w1, b1):
    x_mid = f64(x) + (mxq(f64(attn), 2, "e4m3") @ mxq(f64(wo), 0, "e4m3")) + f64(bo)
    h = rms_norm(x_mid, f64(mlp_norm_w))
    g = gelu_erf((mxq(h, 2, "e4m3") @ mxq(f64(w1), 0, "e4m3")) + f64(b1))
    return x_mid, g

@@ -1,0 +1,222 @@
+from contextlib import ExitStack
+
+import concourse.mybir as mybir
+from concourse.masks import make_identity
+
+F32 = mybir.dt.float32
+BF16 = mybir.dt.bfloat16
+U32 = mybir.dt.uint32
+U8 = mybir.dt.uint8
+FP8X4 = mybir.dt.float8_e4m3fn_x4
+ALU = mybir.AluOpType
+ACT = mybir.ActivationFunctionType
+
+P = 128
+PACK = 4
+K_PASS = P * PACK
+BANK = 512
+
+TOKENS = 4 * 256
+E = 1024
+D = 1024
+F = 4096
+EPS = 1e-6
+
+TOKEN_TILES = TOKENS // P
+PASSES = D // K_PASS
+UNIT = 1024
+QUARTERS = F // UNIT
+
+FLOPS = 2 * TOKENS * E * D + 2 * TOKENS * D * F
+
+
+def tile_tinyblock_pb_kernel(tc, attn, x, wo, bo, mlp_norm_w, w1, b1, out_0, out_1):
+    nc = tc.nc
+    attn_rows = attn.flatten_outer_dims()
+    x_rows = x.flatten_outer_dims()
+    x_mid_rows = out_0.flatten_outer_dims()
+    g_rows = out_1.flatten_outer_dims()
+
+    with ExitStack() as stack:
+        keep = stack.enter_context(tc.tile_pool(name="keep", bufs=1))
+        raw_pool = stack.enter_context(tc.tile_pool(name="raw", bufs=5))
+        grouped_pool = stack.enter_context(tc.tile_pool(name="grouped", bufs=3))
+        work = stack.enter_context(tc.tile_pool(name="work", bufs=2))
+        result = stack.enter_context(tc.tile_pool(name="result", bufs=5))
+        psum_t = stack.enter_context(tc.psum_pool(name="psum_t", bufs=1))
+        psum_1 = stack.enter_context(tc.psum_pool(name="psum_1", bufs=2))
+        psum_2 = stack.enter_context(tc.psum_pool(name="psum_2", bufs=4))
+
+        ident_f32 = keep.tile([P, P], F32)
+        make_identity(nc, ident_f32[:])
+        ident_bf16 = keep.tile([P, P], BF16)
+        make_identity(nc, ident_bf16[:])
+        minus_half = keep.tile([P, 1], F32)
+        nc.vector.memset(minus_half[:], -0.5)
+
+        wo_codes = keep.tile([P, PASSES, D], U32, align_bytes=64)
+        wo_scales = keep.tile([P, PASSES, D], U8, align_bytes=64)
+        w1_codes = keep.tile([P, PASSES, F], U32, align_bytes=64)
+        w1_scales = keep.tile([P, PASSES, F], U8, align_bytes=64)
+        h_codes = keep.tile([P, TOKEN_TILES, PASSES * P], U32, align_bytes=64)
+        h_scales = keep.tile([P, TOKEN_TILES, PASSES * P], U8, align_bytes=64)
+
+        attn_sb = [keep.tile([P, E], BF16, name="attn%d" % i) for i in range(TOKEN_TILES)]
+        x_sb = [keep.tile([P, D], BF16, name="x%d" % i) for i in range(TOKEN_TILES)]
+        bo_all = keep.tile([P, D], BF16)
+        gain_all = keep.tile([P, D], BF16)
+        b1_all = keep.tile([P, F], BF16)
+
+        def load_tokens(i):
+            rows = slice(i * P, (i + 1) * P)
+            nc.sync.dma_start(out=attn_sb[i][:], in_=attn_rows[rows, :])
+            nc.sync.dma_start(out=x_sb[i][:], in_=x_rows[rows, :])
+
+        def load_wo_unit(g):
+            raw = raw_pool.tile([P, PACK, UNIT], BF16, name="wo_raw%d" % g, tag="raw")
+            for u in range(2):
+                first = g * K_PASS + u * 2 * P
+                nc.sync.dma_start(
+                    out=raw[:, 2 * u : 2 * u + 2, :],
+                    in_=wo[first : first + 2 * P, :].rearrange("(p e) n -> p e n", e=2),
+                )
+            return raw
+
+        def load_w1_unit(q, g):
+            raw = raw_pool.tile([P, PACK, UNIT], BF16, name="w1_raw%d_%d" % (q, g), tag="raw")
+            nc.sync.dma_start(
+                out=raw[:],
+                in_=w1[g * K_PASS : (g + 1) * K_PASS, q * UNIT : (q + 1) * UNIT].rearrange(
+                    "(t p) n -> p t n", p=P
+                ),
+            )
+            return raw
+
+        w1_units = [(q, g) for q in range(QUARTERS) for g in range(PASSES)]
+
+        nc.sync.dma_start(out=attn_sb[0][:], in_=attn_rows[0:P, :])
+        wo_raw = [load_wo_unit(g) for g in range(PASSES)]
+        nc.sync.dma_start(out=bo_all[:], in_=bo.partition_broadcast(P))
+        nc.sync.dma_start(out=x_sb[0][:], in_=x_rows[0:P, :])
+        nc.sync.dma_start(out=gain_all[:], in_=mlp_norm_w.partition_broadcast(P))
+        w1_raw = []
+        for i in range(1, TOKEN_TILES):
+            load_tokens(i)
+            w1_raw.append(load_w1_unit(*w1_units[i - 1]))
+            if i == 2:
+                nc.sync.dma_start(out=b1_all[:], in_=b1.partition_broadcast(P))
+        w1_raw.append(load_w1_unit(*w1_units[TOKEN_TILES - 1]))
+
+        def quantise_weight_unit(raw, codes, scales, vector_cols):
+            grouped = grouped_pool.tile([P, UNIT, PACK], BF16, align_bytes=64)
+            nc.vector.tensor_copy(
+                out=grouped[:, 0:vector_cols, :].rearrange("p (c i) t -> p c t i", i=4),
+                in_=raw[:, :, 0:vector_cols].rearrange("p t (c i) -> p c t i", i=4),
+            )
+            nc.scalar.copy(
+                out=grouped[:, vector_cols:UNIT, :].rearrange("p (c i) t -> p c t i", i=4),
+                in_=raw[:, :, vector_cols:UNIT].rearrange("p t (c i) -> p c t i", i=4),
+            )
+            nc.vector.quantize_mx(
+                out=codes.bitcast(FP8X4),
+                scales=scales,
+                in_=grouped[:].rearrange("p w t -> p (w t)"),
+            )
+
+        def first_stage(i):
+            rows = slice(i * P, (i + 1) * P)
+            words = attn_sb[i][:].bitcast(F32)
+            attn_t = psum_t.tile([P, PACK, P], F32)
+            for j in range(PACK):
+                nc.tensor.transpose(attn_t[:, j, :], words[:, j * P : (j + 1) * P], ident_f32[:])
+            attn_grouped = work.tile([P, PASSES * P * PACK], BF16, align_bytes=64)
+            nc.scalar.copy(
+                out=attn_grouped[:].bitcast(F32).rearrange("p (g r u) -> p g r u", g=PASSES, u=2),
+                in_=attn_t[:].rearrange("p (g u) r -> p g r u", u=2),
+            )
+            attn_codes = work.tile([P, PASSES * P], U32, align_bytes=64)
+            attn_scales = work.tile([P, PASSES * P], U8, align_bytes=64)
+            nc.vector.quantize_mx(
+                out=attn_codes[:].bitcast(FP8X4), scales=attn_scales[:], in_=attn_grouped[:]
+            )
+            x_bo = work.tile([P, D], F32)
+            nc.vector.tensor_tensor(out=x_bo[:], in0=x_sb[i][:], in1=bo_all[:], op=ALU.add)
+
+            x_mid = work.tile([P, D], F32, bufs=3)
+            for n in range(D // BANK):
+                cols = slice(n * BANK, (n + 1) * BANK)
+                acc = psum_1.tile([P, BANK], F32)
+                for g in range(PASSES):
+                    toks = slice(g * P, (g + 1) * P)
+                    nc.tensor.matmul_mx(
+                        out=acc[:],
+                        lhsT=attn_codes[:, toks].bitcast(FP8X4),
+                        lhsT_scale=attn_scales[:, toks],
+                        rhs=wo_codes[:, g, cols].bitcast(FP8X4),
+                        rhs_scale=wo_scales[:, g, cols],
+                        start=(g == 0),
+                        stop=(g == PASSES - 1),
+                    )
+                nc.vector.tensor_tensor(out=x_mid[:, cols], in0=acc[:], in1=x_bo[:, cols], op=ALU.add)
+            nc.sync.dma_start(out=x_mid_rows[rows, :], in_=x_mid[:])
+
+            squares = work.tile([P, D], BF16)
+            mean_sq = work.tile([P, 1], F32)
+            nc.scalar.activation(
+                out=squares[:], in_=x_mid[:], func=ACT.Square, scale=D**-0.5, accum_out=mean_sq[:]
+            )
+            mean_eps = work.tile([P, 1], F32)
+            nc.gpsimd.tensor_scalar(
+                out=mean_eps[:], in0=mean_sq[:], scalar1=EPS, scalar2=None, op0=ALU.add
+            )
+            inv_rms = work.tile([P, 1], F32)
+            nc.gpsimd.tensor_tensor(out=inv_rms[:], in0=mean_eps[:], in1=minus_half[:], op=ALU.pow)
+
+            h = work.tile([P, D], BF16)
+            nc.vector.scalar_tensor_tensor(
+                out=h[:], in0=x_mid[:], scalar=inv_rms[:, 0:1], in1=gain_all[:], op0=ALU.mult, op1=ALU.mult
+            )
+            h_t = psum_t.tile([P, PASSES * PACK, P], BF16)
+            for j in range(PASSES * PACK):
+                nc.tensor.transpose(h_t[:, j, :], h[:, j * P : (j + 1) * P], ident_bf16[:])
+            h_grouped = work.tile([P, PASSES, P, PACK], BF16, align_bytes=64)
+            nc.scalar.copy(out=h_grouped[:], in_=h_t[:].rearrange("p (g t) r -> p g r t", t=PACK))
+            nc.vector.quantize_mx(
+                out=h_codes[:, i, :].bitcast(FP8X4),
+                scales=h_scales[:, i, :],
+                in_=h_grouped[:].rearrange("p g r t -> p (g r t)"),
+            )
+
+        def second_stage(i, q):
+            rows = slice(i * P, (i + 1) * P)
+            g_tile = result.tile([P, UNIT], F32)
+            for n in range(UNIT // BANK):
+                cols = slice(q * UNIT + n * BANK, q * UNIT + (n + 1) * BANK)
+                acc = psum_2.tile([P, BANK], F32)
+                for g in range(PASSES):
+                    toks = slice(g * P, (g + 1) * P)
+                    nc.tensor.matmul_mx(
+                        out=acc[:],
+                        lhsT=h_codes[:, i, toks].bitcast(FP8X4),
+                        lhsT_scale=h_scales[:, i, toks],
+                        rhs=w1_codes[:, g, cols].bitcast(FP8X4),
+                        rhs_scale=w1_scales[:, g, cols],
+                        start=(g == 0),
+                        stop=(g == PASSES - 1),
+                    )
+                nc.vector.tensor_tensor(
+                    out=g_tile[:, n * BANK : (n + 1) * BANK], in0=acc[:], in1=b1_all[:, cols], op=ALU.add
+                )
+            nc.scalar.activation(out=g_tile[:], in_=g_tile[:], func=ACT.Gelu)
+            nc.sync.dma_start(out=g_rows[rows, q * UNIT : (q + 1) * UNIT], in_=g_tile[:])
+
+        for g in range(PASSES):
+            quantise_weight_unit(wo_raw[g], wo_codes[:, g, :], wo_scales[:, g, :], UNIT // 2)
+        for i in range(TOKEN_TILES):
+            first_stage(i)
+            q, g = w1_units[i]
+            unit_cols = slice(q * UNIT, (q + 1) * UNIT)
+            quantise_weight_unit(w1_raw[i], w1_codes[:, g, unit_cols], w1_scales[:, g, unit_cols], UNIT // 4)
+        for q in range(QUARTERS):
+            for i in range(TOKEN_TILES):
+                second_stage(i, q)

@@ -27,6 +27,9 @@ PASSES = D // K_PASS
 UNIT = 1024
 QUARTERS = F // UNIT
 
+WEIGHT_UNITS = PASSES * (D // UNIT) + PASSES * QUARTERS
+LAG = 3
+
 FLOPS = 2 * TOKENS * E * D + 2 * TOKENS * D * F
 
 
@@ -42,35 +45,35 @@ def tile_tinyblock_pb_kernel(tc, attn, x, wo, bo, mlp_norm_w, w1, b1, out_0, out
         raw_pool = stack.enter_context(tc.tile_pool(name="raw", bufs=5))
         grouped_pool = stack.enter_context(tc.tile_pool(name="grouped", bufs=3))
         work = stack.enter_context(tc.tile_pool(name="work", bufs=2))
-        result = stack.enter_context(tc.tile_pool(name="result", bufs=5))
+        result = stack.enter_context(tc.tile_pool(name="result", bufs=6))
         psum_t = stack.enter_context(tc.psum_pool(name="psum_t", bufs=1))
         psum_1 = stack.enter_context(tc.psum_pool(name="psum_1", bufs=2))
         psum_2 = stack.enter_context(tc.psum_pool(name="psum_2", bufs=4))
 
+        minus_half = keep.tile([P, 1], F32)
+        nc.vector.memset(minus_half[:], -0.5)
+        table_warm = keep.tile([P, 1], F32)
+        nc.scalar.activation(out=table_warm[:], in_=minus_half[:], func=ACT.Gelu)
         ident_f32 = keep.tile([P, P], F32)
         make_identity(nc, ident_f32[:])
         ident_bf16 = keep.tile([P, P], BF16)
         make_identity(nc, ident_bf16[:])
-        minus_half = keep.tile([P, 1], F32)
-        nc.vector.memset(minus_half[:], -0.5)
 
         wo_codes = keep.tile([P, PASSES, D], U32, align_bytes=64)
         wo_scales = keep.tile([P, PASSES, D], U8, align_bytes=64)
         w1_codes = keep.tile([P, PASSES, F], U32, align_bytes=64)
         w1_scales = keep.tile([P, PASSES, F], U8, align_bytes=64)
-        h_codes = keep.tile([P, TOKEN_TILES, PASSES * P], U32, align_bytes=64)
-        h_scales = keep.tile([P, TOKEN_TILES, PASSES * P], U8, align_bytes=64)
 
-        attn_sb = [keep.tile([P, E], BF16, name="attn%d" % i) for i in range(TOKEN_TILES)]
-        x_sb = [keep.tile([P, D], BF16, name="x%d" % i) for i in range(TOKEN_TILES)]
+        attn_sb = [keep.tile([P, E], BF16, name="attn%d" % j) for j in range(TOKEN_TILES)]
+        x_sb = [keep.tile([P, D], BF16, name="x%d" % j) for j in range(TOKEN_TILES)]
         bo_all = keep.tile([P, D], BF16)
         gain_all = keep.tile([P, D], BF16)
         b1_all = keep.tile([P, F], BF16)
 
-        def load_tokens(i):
-            rows = slice(i * P, (i + 1) * P)
-            nc.sync.dma_start(out=attn_sb[i][:], in_=attn_rows[rows, :])
-            nc.sync.dma_start(out=x_sb[i][:], in_=x_rows[rows, :])
+        def load_tokens(j):
+            rows = slice(j * P, (j + 1) * P)
+            nc.sync.dma_start(out=attn_sb[j][:], in_=attn_rows[rows, :])
+            nc.sync.dma_start(out=x_sb[j][:], in_=x_rows[rows, :])
 
         def load_wo_unit(g):
             raw = raw_pool.tile([P, PACK, UNIT], BF16, name="wo_raw%d" % g, tag="raw")
@@ -92,113 +95,142 @@ def tile_tinyblock_pb_kernel(tc, attn, x, wo, bo, mlp_norm_w, w1, b1, out_0, out
             )
             return raw
 
-        w1_units = [(q, g) for q in range(QUARTERS) for g in range(PASSES)]
-
+        units = []
         nc.sync.dma_start(out=attn_sb[0][:], in_=attn_rows[0:P, :])
-        wo_raw = [load_wo_unit(g) for g in range(PASSES)]
+        for g in range(PASSES):
+            units.append((load_wo_unit(g), wo_codes[:, g, :], wo_scales[:, g, :]))
         nc.sync.dma_start(out=bo_all[:], in_=bo.partition_broadcast(P))
         nc.sync.dma_start(out=x_sb[0][:], in_=x_rows[0:P, :])
+        for j in range(1, LAG):
+            load_tokens(j)
         nc.sync.dma_start(out=gain_all[:], in_=mlp_norm_w.partition_broadcast(P))
-        w1_raw = []
-        for i in range(1, TOKEN_TILES):
-            load_tokens(i)
-            w1_raw.append(load_w1_unit(*w1_units[i - 1]))
-            if i == 2:
+        for q in range(QUARTERS):
+            cols = slice(q * UNIT, (q + 1) * UNIT)
+            for g in range(PASSES):
+                units.append((load_w1_unit(q, g), w1_codes[:, g, cols], w1_scales[:, g, cols]))
+            if q == 0:
                 nc.sync.dma_start(out=b1_all[:], in_=b1.partition_broadcast(P))
-        w1_raw.append(load_w1_unit(*w1_units[TOKEN_TILES - 1]))
+        for j in range(LAG, TOKEN_TILES):
+            load_tokens(j)
 
-        def quantise_weight_unit(raw, codes, scales, vector_cols):
-            grouped = grouped_pool.tile([P, UNIT, PACK], BF16, align_bytes=64)
-            nc.vector.tensor_copy(
-                out=grouped[:, 0:vector_cols, :].rearrange("p (c i) t -> p c t i", i=4),
-                in_=raw[:, :, 0:vector_cols].rearrange("p t (c i) -> p c t i", i=4),
-            )
-            nc.scalar.copy(
-                out=grouped[:, vector_cols:UNIT, :].rearrange("p (c i) t -> p c t i", i=4),
-                in_=raw[:, :, vector_cols:UNIT].rearrange("p t (c i) -> p c t i", i=4),
-            )
-            nc.vector.quantize_mx(
-                out=codes.bitcast(FP8X4),
-                scales=scales,
-                in_=grouped[:].rearrange("p w t -> p (w t)"),
-            )
+        grouped_tiles = []
 
-        def first_stage(i):
-            rows = slice(i * P, (i + 1) * P)
-            words = attn_sb[i][:].bitcast(F32)
+        def weight_step(s):
+            if s < WEIGHT_UNITS:
+                raw = units[s][0]
+                grouped = grouped_pool.tile([P, UNIT, PACK], BF16, align_bytes=64)
+                half = UNIT // 2
+                nc.vector.tensor_copy(
+                    out=grouped[:, 0:half, :].rearrange("p (c i) t -> p c t i", i=4),
+                    in_=raw[:, :, 0:half].rearrange("p t (c i) -> p c t i", i=4),
+                )
+                nc.scalar.copy(
+                    out=grouped[:, half:UNIT, :].rearrange("p (c i) t -> p c t i", i=4),
+                    in_=raw[:, :, half:UNIT].rearrange("p t (c i) -> p c t i", i=4),
+                )
+                grouped_tiles.append(grouped)
+            if s >= 1:
+                nc.vector.quantize_mx(
+                    out=units[s - 1][1].bitcast(FP8X4),
+                    scales=units[s - 1][2],
+                    in_=grouped_tiles[s - 1][:].rearrange("p w t -> p (w t)"),
+                )
+
+        attn_grouped, attn_mx, x_bo, acc_1, x_mid, inv_rms, h, h_grouped, h_mx = ({} for n in range(9))
+
+        def transpose_attn(j):
+            words = attn_sb[j][:].bitcast(F32)
             attn_t = psum_t.tile([P, PACK, P], F32)
-            for j in range(PACK):
-                nc.tensor.transpose(attn_t[:, j, :], words[:, j * P : (j + 1) * P], ident_f32[:])
-            attn_grouped = work.tile([P, PASSES * P * PACK], BF16, align_bytes=64)
+            for w in range(PACK):
+                nc.tensor.transpose(attn_t[:, w, :], words[:, w * P : (w + 1) * P], ident_f32[:])
+            grouped = work.tile([P, PASSES * P * PACK], BF16, align_bytes=64, name="attn_grouped")
             nc.scalar.copy(
-                out=attn_grouped[:].bitcast(F32).rearrange("p (g r u) -> p g r u", g=PASSES, u=2),
+                out=grouped[:].bitcast(F32).rearrange("p (g r u) -> p g r u", g=PASSES, u=2),
                 in_=attn_t[:].rearrange("p (g u) r -> p g r u", u=2),
             )
-            attn_codes = work.tile([P, PASSES * P], U32, align_bytes=64)
-            attn_scales = work.tile([P, PASSES * P], U8, align_bytes=64)
-            nc.vector.quantize_mx(
-                out=attn_codes[:].bitcast(FP8X4), scales=attn_scales[:], in_=attn_grouped[:]
-            )
-            x_bo = work.tile([P, D], F32)
-            nc.vector.tensor_tensor(out=x_bo[:], in0=x_sb[i][:], in1=bo_all[:], op=ALU.add)
+            attn_grouped[j] = grouped
 
-            x_mid = work.tile([P, D], F32, bufs=3)
+        def quantise_attn(j):
+            codes = work.tile([P, PASSES * P], U32, align_bytes=64, name="attn_codes")
+            scales = work.tile([P, PASSES * P], U8, align_bytes=64, name="attn_scales")
+            nc.vector.quantize_mx(out=codes[:].bitcast(FP8X4), scales=scales[:], in_=attn_grouped[j][:])
+            attn_mx[j] = (codes, scales)
+
+        def add_bo_to_x(j):
+            total = work.tile([P, D], F32, name="x_bo")
+            nc.gpsimd.tensor_tensor(out=total[:], in0=x_sb[j][:], in1=bo_all[:], op=ALU.add)
+            x_bo[j] = total
+
+        def first_matmul(j):
+            codes, scales = attn_mx[j]
+            acc_1[j] = []
             for n in range(D // BANK):
                 cols = slice(n * BANK, (n + 1) * BANK)
-                acc = psum_1.tile([P, BANK], F32)
+                acc = psum_1.tile([P, BANK], F32, name="acc_1")
                 for g in range(PASSES):
                     toks = slice(g * P, (g + 1) * P)
                     nc.tensor.matmul_mx(
                         out=acc[:],
-                        lhsT=attn_codes[:, toks].bitcast(FP8X4),
-                        lhsT_scale=attn_scales[:, toks],
+                        lhsT=codes[:, toks].bitcast(FP8X4),
+                        lhsT_scale=scales[:, toks],
                         rhs=wo_codes[:, g, cols].bitcast(FP8X4),
                         rhs_scale=wo_scales[:, g, cols],
                         start=(g == 0),
                         stop=(g == PASSES - 1),
                     )
-                nc.vector.tensor_tensor(out=x_mid[:, cols], in0=acc[:], in1=x_bo[:, cols], op=ALU.add)
-            nc.sync.dma_start(out=x_mid_rows[rows, :], in_=x_mid[:])
+                acc_1[j].append(acc)
 
+        def residual_and_rms(j):
+            total = work.tile([P, D], F32, name="x_mid", bufs=3)
+            for n in range(D // BANK):
+                cols = slice(n * BANK, (n + 1) * BANK)
+                nc.vector.tensor_tensor(out=total[:, cols], in0=acc_1[j][n][:], in1=x_bo[j][:, cols], op=ALU.add)
+            nc.sync.dma_start(out=x_mid_rows[j * P : (j + 1) * P, :], in_=total[:])
             squares = work.tile([P, D], BF16)
             mean_sq = work.tile([P, 1], F32)
-            nc.scalar.activation(
-                out=squares[:], in_=x_mid[:], func=ACT.Square, scale=D**-0.5, accum_out=mean_sq[:]
-            )
+            nc.scalar.activation(out=squares[:], in_=total[:], func=ACT.Square, scale=D**-0.5, accum_out=mean_sq[:])
             mean_eps = work.tile([P, 1], F32)
-            nc.gpsimd.tensor_scalar(
-                out=mean_eps[:], in0=mean_sq[:], scalar1=EPS, scalar2=None, op0=ALU.add
-            )
-            inv_rms = work.tile([P, 1], F32)
-            nc.gpsimd.tensor_tensor(out=inv_rms[:], in0=mean_eps[:], in1=minus_half[:], op=ALU.pow)
+            nc.gpsimd.tensor_scalar(out=mean_eps[:], in0=mean_sq[:], scalar1=EPS, scalar2=None, op0=ALU.add)
+            power = work.tile([P, 1], F32, name="inv_rms")
+            nc.gpsimd.tensor_tensor(out=power[:], in0=mean_eps[:], in1=minus_half[:], op=ALU.pow)
+            x_mid[j] = total
+            inv_rms[j] = power
 
-            h = work.tile([P, D], BF16)
+        def normalise(j):
+            normed = work.tile([P, D], BF16, name="h")
             nc.vector.scalar_tensor_tensor(
-                out=h[:], in0=x_mid[:], scalar=inv_rms[:, 0:1], in1=gain_all[:], op0=ALU.mult, op1=ALU.mult
+                out=normed[:], in0=x_mid[j][:], scalar=inv_rms[j][:, 0:1], in1=gain_all[:], op0=ALU.mult, op1=ALU.mult
             )
-            h_t = psum_t.tile([P, PASSES * PACK, P], BF16)
-            for j in range(PASSES * PACK):
-                nc.tensor.transpose(h_t[:, j, :], h[:, j * P : (j + 1) * P], ident_bf16[:])
-            h_grouped = work.tile([P, PASSES, P, PACK], BF16, align_bytes=64)
-            nc.scalar.copy(out=h_grouped[:], in_=h_t[:].rearrange("p (g t) r -> p g r t", t=PACK))
-            nc.vector.quantize_mx(
-                out=h_codes[:, i, :].bitcast(FP8X4),
-                scales=h_scales[:, i, :],
-                in_=h_grouped[:].rearrange("p g r t -> p (g r t)"),
-            )
+            h[j] = normed
 
-        def second_stage(i, q):
-            rows = slice(i * P, (i + 1) * P)
+        def transpose_h(j):
+            h_t = psum_t.tile([P, PASSES * PACK, P], BF16)
+            for w in range(PASSES * PACK):
+                nc.tensor.transpose(h_t[:, w, :], h[j][:, w * P : (w + 1) * P], ident_bf16[:])
+            grouped = work.tile([P, PASSES, P, PACK], BF16, align_bytes=64, name="h_grouped")
+            nc.scalar.copy(out=grouped[:], in_=h_t[:].rearrange("p (g t) r -> p g r t", t=PACK))
+            h_grouped[j] = grouped
+
+        def quantise_h(j):
+            codes = work.tile([P, PASSES * P], U32, align_bytes=64, name="h_codes")
+            scales = work.tile([P, PASSES * P], U8, align_bytes=64, name="h_scales")
+            nc.vector.quantize_mx(
+                out=codes[:].bitcast(FP8X4), scales=scales[:], in_=h_grouped[j][:].rearrange("p g r t -> p (g r t)")
+            )
+            h_mx[j] = (codes, scales)
+
+        def second_stage(j, q):
+            codes, scales = h_mx[j]
             g_tile = result.tile([P, UNIT], F32)
             for n in range(UNIT // BANK):
                 cols = slice(q * UNIT + n * BANK, q * UNIT + (n + 1) * BANK)
-                acc = psum_2.tile([P, BANK], F32)
+                acc = psum_2.tile([P, BANK], F32, name="acc_2")
                 for g in range(PASSES):
                     toks = slice(g * P, (g + 1) * P)
                     nc.tensor.matmul_mx(
                         out=acc[:],
-                        lhsT=h_codes[:, i, toks].bitcast(FP8X4),
-                        lhsT_scale=h_scales[:, i, toks],
+                        lhsT=codes[:, toks].bitcast(FP8X4),
+                        lhsT_scale=scales[:, toks],
                         rhs=w1_codes[:, g, cols].bitcast(FP8X4),
                         rhs_scale=w1_scales[:, g, cols],
                         start=(g == 0),
@@ -208,15 +240,34 @@ def tile_tinyblock_pb_kernel(tc, attn, x, wo, bo, mlp_norm_w, w1, b1, out_0, out
                     out=g_tile[:, n * BANK : (n + 1) * BANK], in0=acc[:], in1=b1_all[:, cols], op=ALU.add
                 )
             nc.scalar.activation(out=g_tile[:], in_=g_tile[:], func=ACT.Gelu)
-            nc.sync.dma_start(out=g_rows[rows, q * UNIT : (q + 1) * UNIT], in_=g_tile[:])
+            nc.sync.dma_start(out=g_rows[j * P : (j + 1) * P, q * UNIT : (q + 1) * UNIT], in_=g_tile[:])
 
-        for g in range(PASSES):
-            quantise_weight_unit(wo_raw[g], wo_codes[:, g, :], wo_scales[:, g, :], UNIT // 2)
-        for i in range(TOKEN_TILES):
-            first_stage(i)
-            q, g = w1_units[i]
-            unit_cols = slice(q * UNIT, (q + 1) * UNIT)
-            quantise_weight_unit(w1_raw[i], w1_codes[:, g, unit_cols], w1_scales[:, g, unit_cols], UNIT // 4)
-        for q in range(QUARTERS):
-            for i in range(TOKEN_TILES):
-                second_stage(i, q)
+        def live(j):
+            return 0 <= j < TOKEN_TILES
+
+        steps_a_round = (WEIGHT_UNITS + 1 + LAG - 1) // LAG
+        for i in range(-LAG, TOKEN_TILES):
+            if live(i + 3):
+                transpose_attn(i + 3)
+            if live(i + 1):
+                transpose_h(i + 1)
+            if live(i + 2):
+                residual_and_rms(i + 2)
+            if live(i + 3):
+                add_bo_to_x(i + 3)
+                quantise_attn(i + 3)
+            if live(i + 1):
+                quantise_h(i + 1)
+            if i < 0:
+                first_step = (i + LAG) * steps_a_round
+                for s in range(first_step, min(first_step + steps_a_round, WEIGHT_UNITS + 1)):
+                    weight_step(s)
+            else:
+                for q in range(QUARTERS - 1):
+                    second_stage(i, q)
+            if live(i + 2):
+                normalise(i + 2)
+            if i >= 0:
+                second_stage(i, QUARTERS - 1)
+            if live(i + 3):
+                first_matmul(i + 3)

@@ -28,7 +28,7 @@ UNIT = 1024
 QUARTERS = F // UNIT
 
 WEIGHT_UNITS = PASSES * (D // UNIT) + PASSES * QUARTERS
-LAG = 3
+LAG = 5
 
 FLOPS = 2 * TOKENS * E * D + 2 * TOKENS * D * F
 
@@ -49,6 +49,7 @@ def tile_tinyblock_pb_kernel(tc, attn, x, wo, bo, mlp_norm_w, w1, b1, out_0, out
         psum_t = stack.enter_context(tc.psum_pool(name="psum_t", bufs=1))
         psum_1 = stack.enter_context(tc.psum_pool(name="psum_1", bufs=2))
         psum_2 = stack.enter_context(tc.psum_pool(name="psum_2", bufs=4))
+        stack.enter_context(tc.manual_schedule())
 
         minus_half = keep.tile([P, 1], F32)
         nc.vector.memset(minus_half[:], -0.5)
@@ -96,20 +97,18 @@ def tile_tinyblock_pb_kernel(tc, attn, x, wo, bo, mlp_norm_w, w1, b1, out_0, out
             return raw
 
         units = []
-        nc.sync.dma_start(out=attn_sb[0][:], in_=attn_rows[0:P, :])
+        nc.scalar.dma_start(out=bo_all[:], in_=bo.partition_broadcast(P))
+        nc.scalar.dma_start(out=gain_all[:], in_=mlp_norm_w.partition_broadcast(P))
+        load_tokens(0)
         for g in range(PASSES):
             units.append((load_wo_unit(g), wo_codes[:, g, :], wo_scales[:, g, :]))
-        nc.sync.dma_start(out=bo_all[:], in_=bo.partition_broadcast(P))
-        nc.sync.dma_start(out=x_sb[0][:], in_=x_rows[0:P, :])
-        for j in range(1, LAG):
-            load_tokens(j)
-        nc.sync.dma_start(out=gain_all[:], in_=mlp_norm_w.partition_broadcast(P))
         for q in range(QUARTERS):
             cols = slice(q * UNIT, (q + 1) * UNIT)
             for g in range(PASSES):
                 units.append((load_w1_unit(q, g), w1_codes[:, g, cols], w1_scales[:, g, cols]))
-            if q == 0:
-                nc.sync.dma_start(out=b1_all[:], in_=b1.partition_broadcast(P))
+                if len(units) - PASSES < LAG:
+                    load_tokens(len(units) - PASSES)
+        nc.sync.dma_start(out=b1_all[:], in_=b1.partition_broadcast(P))
         for j in range(LAG, TOKEN_TILES):
             load_tokens(j)
 
@@ -245,29 +244,34 @@ def tile_tinyblock_pb_kernel(tc, attn, x, wo, bo, mlp_norm_w, w1, b1, out_0, out
         def live(j):
             return 0 <= j < TOKEN_TILES
 
-        steps_a_round = (WEIGHT_UNITS + 1 + LAG - 1) // LAG
-        for i in range(-LAG, TOKEN_TILES):
-            if live(i + 3):
-                transpose_attn(i + 3)
-            if live(i + 1):
-                transpose_h(i + 1)
-            if live(i + 2):
-                residual_and_rms(i + 2)
-            if live(i + 3):
-                add_bo_to_x(i + 3)
-                quantise_attn(i + 3)
-            if live(i + 1):
-                quantise_h(i + 1)
-            if i < 0:
-                first_step = (i + LAG) * steps_a_round
-                for s in range(first_step, min(first_step + steps_a_round, WEIGHT_UNITS + 1)):
-                    weight_step(s)
+        def slot(i, k):
+            if i >= 0:
+                second_stage(i, k)
             else:
-                for q in range(QUARTERS - 1):
-                    second_stage(i, q)
+                r = i + LAG
+                first_step = -(-(WEIGHT_UNITS + 1) * r // LAG)
+                next_first = -(-(WEIGHT_UNITS + 1) * (r + 1) // LAG)
+                if first_step + k < next_first:
+                    weight_step(first_step + k)
+
+        for i in range(-LAG, TOKEN_TILES):
             if live(i + 2):
                 normalise(i + 2)
-            if i >= 0:
-                second_stage(i, QUARTERS - 1)
+            slot(i, 0)
             if live(i + 3):
-                first_matmul(i + 3)
+                residual_and_rms(i + 3)
+            if live(i + 4):
+                add_bo_to_x(i + 4)
+            slot(i, 1)
+            if live(i + 4):
+                quantise_attn(i + 4)
+            if live(i + 1):
+                quantise_h(i + 1)
+            slot(i, 2)
+            if live(i + 5):
+                transpose_attn(i + 5)
+            if live(i + 2):
+                transpose_h(i + 2)
+            slot(i, 3)
+            if live(i + 4):
+                first_matmul(i + 4)

@@ -7,6 +7,7 @@ F32 = mybir.dt.float32
 BF16 = mybir.dt.bfloat16
 U32 = mybir.dt.uint32
 U8 = mybir.dt.uint8
+I32 = mybir.dt.int32
 FP8X4 = mybir.dt.float8_e4m3fn_x4
 ALU = mybir.AluOpType
 ACT = mybir.ActivationFunctionType
@@ -28,7 +29,7 @@ UNIT = 1024
 QUARTERS = F // UNIT
 
 WEIGHT_UNITS = PASSES * (D // UNIT) + PASSES * QUARTERS
-LAG = 5
+LAG = 3
 
 FLOPS = 2 * TOKENS * E * D + 2 * TOKENS * D * F
 
@@ -45,11 +46,9 @@ def tile_tinyblock_pb_kernel(tc, attn, x, wo, bo, mlp_norm_w, w1, b1, out_0, out
         raw_pool = stack.enter_context(tc.tile_pool(name="raw", bufs=5))
         grouped_pool = stack.enter_context(tc.tile_pool(name="grouped", bufs=3))
         work = stack.enter_context(tc.tile_pool(name="work", bufs=2))
-        result = stack.enter_context(tc.tile_pool(name="result", bufs=6))
         psum_t = stack.enter_context(tc.psum_pool(name="psum_t", bufs=1))
         psum_1 = stack.enter_context(tc.psum_pool(name="psum_1", bufs=2))
         psum_2 = stack.enter_context(tc.psum_pool(name="psum_2", bufs=4))
-        stack.enter_context(tc.manual_schedule())
 
         minus_half = keep.tile([P, 1], F32)
         nc.vector.memset(minus_half[:], -0.5)
@@ -60,6 +59,31 @@ def tile_tinyblock_pb_kernel(tc, attn, x, wo, bo, mlp_norm_w, w1, b1, out_0, out
         ident_bf16 = keep.tile([P, P], BF16)
         make_identity(nc, ident_bf16[:])
 
+        bo_all = keep.tile([P, D], BF16)
+        gain_all = keep.tile([P, D], BF16)
+        b1_all = keep.tile([P, F], BF16)
+        ones = keep.tile([P, P], BF16)
+        nc.vector.memset(ones[:], 1.0)
+        with tc.tile_pool(name="setup", bufs=1) as setup:
+            for label, vector, everywhere in (("bo", bo, bo_all), ("gain", mlp_norm_w, gain_all), ("b1", b1, b1_all)):
+                width = vector.shape[0]
+                row = setup.tile([P, width], BF16, name="row_" + label)
+                nc.vector.memset(row[:].bitcast(I32), 0)
+                nc.sync.dma_start(out=row[0:1, :], in_=vector.unsqueeze(0))
+                for c in range(width // (2 * BANK)):
+                    spread = psum_2.tile([P, 2 * BANK], BF16, name="spread", tag="acc_2")
+                    for n in range(2):
+                        cols = slice(n * BANK, (n + 1) * BANK)
+                        nc.tensor.matmul(
+                            out=spread[:, cols],
+                            lhsT=ones[:],
+                            rhs=row[:, c * 2 * BANK + n * BANK : c * 2 * BANK + (n + 1) * BANK],
+                            start=True,
+                            stop=True,
+                        )
+                    nc.scalar.copy(out=everywhere[:, c * 2 * BANK : (c + 1) * 2 * BANK], in_=spread[:])
+        result = stack.enter_context(tc.tile_pool(name="result", bufs=6))
+
         wo_codes = keep.tile([P, PASSES, D], U32, align_bytes=64)
         wo_scales = keep.tile([P, PASSES, D], U8, align_bytes=64)
         w1_codes = keep.tile([P, PASSES, F], U32, align_bytes=64)
@@ -67,9 +91,6 @@ def tile_tinyblock_pb_kernel(tc, attn, x, wo, bo, mlp_norm_w, w1, b1, out_0, out
 
         attn_sb = [keep.tile([P, E], BF16, name="attn%d" % j) for j in range(TOKEN_TILES)]
         x_sb = [keep.tile([P, D], BF16, name="x%d" % j) for j in range(TOKEN_TILES)]
-        bo_all = keep.tile([P, D], BF16)
-        gain_all = keep.tile([P, D], BF16)
-        b1_all = keep.tile([P, F], BF16)
 
         def load_tokens(j):
             rows = slice(j * P, (j + 1) * P)
@@ -97,18 +118,16 @@ def tile_tinyblock_pb_kernel(tc, attn, x, wo, bo, mlp_norm_w, w1, b1, out_0, out
             return raw
 
         units = []
-        nc.scalar.dma_start(out=bo_all[:], in_=bo.partition_broadcast(P))
-        nc.scalar.dma_start(out=gain_all[:], in_=mlp_norm_w.partition_broadcast(P))
-        load_tokens(0)
+        nc.sync.dma_start(out=attn_sb[0][:], in_=attn_rows[0:P, :])
         for g in range(PASSES):
             units.append((load_wo_unit(g), wo_codes[:, g, :], wo_scales[:, g, :]))
+        nc.sync.dma_start(out=x_sb[0][:], in_=x_rows[0:P, :])
+        for j in range(1, LAG):
+            load_tokens(j)
         for q in range(QUARTERS):
             cols = slice(q * UNIT, (q + 1) * UNIT)
             for g in range(PASSES):
                 units.append((load_w1_unit(q, g), w1_codes[:, g, cols], w1_scales[:, g, cols]))
-                if len(units) - PASSES < LAG:
-                    load_tokens(len(units) - PASSES)
-        nc.sync.dma_start(out=b1_all[:], in_=b1.partition_broadcast(P))
         for j in range(LAG, TOKEN_TILES):
             load_tokens(j)
 
@@ -244,34 +263,29 @@ def tile_tinyblock_pb_kernel(tc, attn, x, wo, bo, mlp_norm_w, w1, b1, out_0, out
         def live(j):
             return 0 <= j < TOKEN_TILES
 
-        def slot(i, k):
-            if i >= 0:
-                second_stage(i, k)
-            else:
-                r = i + LAG
-                first_step = -(-(WEIGHT_UNITS + 1) * r // LAG)
-                next_first = -(-(WEIGHT_UNITS + 1) * (r + 1) // LAG)
-                if first_step + k < next_first:
-                    weight_step(first_step + k)
-
+        steps_a_round = (WEIGHT_UNITS + 1 + LAG - 1) // LAG
         for i in range(-LAG, TOKEN_TILES):
-            if live(i + 2):
-                normalise(i + 2)
-            slot(i, 0)
             if live(i + 3):
-                residual_and_rms(i + 3)
-            if live(i + 4):
-                add_bo_to_x(i + 4)
-            slot(i, 1)
-            if live(i + 4):
-                quantise_attn(i + 4)
+                transpose_attn(i + 3)
+            if live(i + 1):
+                transpose_h(i + 1)
+            if live(i + 2):
+                residual_and_rms(i + 2)
+            if live(i + 3):
+                add_bo_to_x(i + 3)
+                quantise_attn(i + 3)
             if live(i + 1):
                 quantise_h(i + 1)
-            slot(i, 2)
-            if live(i + 5):
-                transpose_attn(i + 5)
+            if i < 0:
+                first_step = (i + LAG) * steps_a_round
+                for s in range(first_step, min(first_step + steps_a_round, WEIGHT_UNITS + 1)):
+                    weight_step(s)
+            else:
+                for q in range(QUARTERS - 1):
+                    second_stage(i, q)
             if live(i + 2):
-                transpose_h(i + 2)
-            slot(i, 3)
-            if live(i + 4):
-                first_matmul(i + 4)
+                normalise(i + 2)
+            if i >= 0:
+                second_stage(i, QUARTERS - 1)
+            if live(i + 3):
+                first_matmul(i + 3)

from contextlib import ExitStack

import concourse.mybir as mybir
from concourse.masks import make_identity

F32 = mybir.dt.float32
BF16 = mybir.dt.bfloat16
U32 = mybir.dt.uint32
U8 = mybir.dt.uint8
I32 = mybir.dt.int32
FP8X4 = mybir.dt.float8_e4m3fn_x4
ALU = mybir.AluOpType
ACT = mybir.ActivationFunctionType

P = 128
PACK = 4
K_PASS = P * PACK
BANK = 512

TOKENS = 4 * 256
E = 1024
D = 1024
F = 4096
EPS = 1e-6

TOKEN_TILES = TOKENS // P
PASSES = D // K_PASS
UNIT = 1024
QUARTERS = F // UNIT

WEIGHT_UNITS = PASSES * (D // UNIT) + PASSES * QUARTERS
LAG = 3

FLOPS = 2 * TOKENS * E * D + 2 * TOKENS * D * F


def tile_tinyblock_pb_kernel(tc, attn, x, wo, bo, mlp_norm_w, w1, b1, out_0, out_1):
    nc = tc.nc
    attn_rows = attn.flatten_outer_dims()
    x_rows = x.flatten_outer_dims()
    x_mid_rows = out_0.flatten_outer_dims()
    g_rows = out_1.flatten_outer_dims()

    with ExitStack() as stack:
        keep = stack.enter_context(tc.tile_pool(name="keep", bufs=1))
        raw_pool = stack.enter_context(tc.tile_pool(name="raw", bufs=5))
        grouped_pool = stack.enter_context(tc.tile_pool(name="grouped", bufs=3))
        work = stack.enter_context(tc.tile_pool(name="work", bufs=2))
        psum_t = stack.enter_context(tc.psum_pool(name="psum_t", bufs=1))
        psum_1 = stack.enter_context(tc.psum_pool(name="psum_1", bufs=2))
        psum_2 = stack.enter_context(tc.psum_pool(name="psum_2", bufs=4))

        minus_half = keep.tile([P, 1], F32)
        nc.vector.memset(minus_half[:], -0.5)
        table_warm = keep.tile([P, 1], F32)
        nc.scalar.activation(out=table_warm[:], in_=minus_half[:], func=ACT.Gelu)
        ident_f32 = keep.tile([P, P], F32)
        make_identity(nc, ident_f32[:])
        ident_bf16 = keep.tile([P, P], BF16)
        make_identity(nc, ident_bf16[:])

        bo_all = keep.tile([P, D], BF16)
        gain_all = keep.tile([P, D], BF16)
        b1_all = keep.tile([P, F], BF16)
        ones = keep.tile([P, P], BF16)
        nc.vector.memset(ones[:], 1.0)
        with tc.tile_pool(name="setup", bufs=1) as setup:
            for label, vector, everywhere in (("bo", bo, bo_all), ("gain", mlp_norm_w, gain_all), ("b1", b1, b1_all)):
                width = vector.shape[0]
                row = setup.tile([P, width], BF16, name="row_" + label)
                nc.vector.memset(row[:].bitcast(I32), 0)
                nc.sync.dma_start(out=row[0:1, :], in_=vector.unsqueeze(0))
                for c in range(width // (2 * BANK)):
                    spread = psum_2.tile([P, 2 * BANK], BF16, name="spread", tag="acc_2")
                    for n in range(2):
                        cols = slice(n * BANK, (n + 1) * BANK)
                        nc.tensor.matmul(
                            out=spread[:, cols],
                            lhsT=ones[:],
                            rhs=row[:, c * 2 * BANK + n * BANK : c * 2 * BANK + (n + 1) * BANK],
                            start=True,
                            stop=True,
                        )
                    nc.scalar.copy(out=everywhere[:, c * 2 * BANK : (c + 1) * 2 * BANK], in_=spread[:])
        result = stack.enter_context(tc.tile_pool(name="result", bufs=6))

        wo_codes = keep.tile([P, PASSES, D], U32, align_bytes=64)
        wo_scales = keep.tile([P, PASSES, D], U8, align_bytes=64)
        w1_codes = keep.tile([P, PASSES, F], U32, align_bytes=64)
        w1_scales = keep.tile([P, PASSES, F], U8, align_bytes=64)

        attn_sb = [keep.tile([P, E], BF16, name="attn%d" % j) for j in range(TOKEN_TILES)]
        x_sb = [keep.tile([P, D], BF16, name="x%d" % j) for j in range(TOKEN_TILES)]

        def load_tokens(j):
            rows = slice(j * P, (j + 1) * P)
            nc.sync.dma_start(out=attn_sb[j][:], in_=attn_rows[rows, :])
            nc.sync.dma_start(out=x_sb[j][:], in_=x_rows[rows, :])

        def load_wo_unit(g):
            raw = raw_pool.tile([P, PACK, UNIT], BF16, name="wo_raw%d" % g, tag="raw")
            for u in range(2):
                first = g * K_PASS + u * 2 * P
                nc.sync.dma_start(
                    out=raw[:, 2 * u : 2 * u + 2, :],
                    in_=wo[first : first + 2 * P, :].rearrange("(p e) n -> p e n", e=2),
                )
            return raw

        def load_w1_unit(q, g):
            raw = raw_pool.tile([P, PACK, UNIT], BF16, name="w1_raw%d_%d" % (q, g), tag="raw")
            nc.sync.dma_start(
                out=raw[:],
                in_=w1[g * K_PASS : (g + 1) * K_PASS, q * UNIT : (q + 1) * UNIT].rearrange(
                    "(t p) n -> p t n", p=P
                ),
            )
            return raw

        units = []
        nc.sync.dma_start(out=attn_sb[0][:], in_=attn_rows[0:P, :])
        for g in range(PASSES):
            units.append((load_wo_unit(g), wo_codes[:, g, :], wo_scales[:, g, :]))
        nc.sync.dma_start(out=x_sb[0][:], in_=x_rows[0:P, :])
        for j in range(1, LAG):
            load_tokens(j)
        for q in range(QUARTERS):
            cols = slice(q * UNIT, (q + 1) * UNIT)
            for g in range(PASSES):
                units.append((load_w1_unit(q, g), w1_codes[:, g, cols], w1_scales[:, g, cols]))
        for j in range(LAG, TOKEN_TILES):
            load_tokens(j)

        grouped_tiles = []

        def weight_step(s):
            if s < WEIGHT_UNITS:
                raw = units[s][0]
                grouped = grouped_pool.tile([P, UNIT, PACK], BF16, align_bytes=64)
                half = UNIT // 2
                nc.vector.tensor_copy(
                    out=grouped[:, 0:half, :].rearrange("p (c i) t -> p c t i", i=4),
                    in_=raw[:, :, 0:half].rearrange("p t (c i) -> p c t i", i=4),
                )
                nc.scalar.copy(
                    out=grouped[:, half:UNIT, :].rearrange("p (c i) t -> p c t i", i=4),
                    in_=raw[:, :, half:UNIT].rearrange("p t (c i) -> p c t i", i=4),
                )
                grouped_tiles.append(grouped)
            if s >= 1:
                nc.vector.quantize_mx(
                    out=units[s - 1][1].bitcast(FP8X4),
                    scales=units[s - 1][2],
                    in_=grouped_tiles[s - 1][:].rearrange("p w t -> p (w t)"),
                )

        attn_grouped, attn_mx, x_bo, acc_1, x_mid, inv_rms, h, h_grouped, h_mx = ({} for n in range(9))

        def transpose_attn(j):
            words = attn_sb[j][:].bitcast(F32)
            attn_t = psum_t.tile([P, PACK, P], F32)
            for w in range(PACK):
                nc.tensor.transpose(attn_t[:, w, :], words[:, w * P : (w + 1) * P], ident_f32[:])
            grouped = work.tile([P, PASSES * P * PACK], BF16, align_bytes=64, name="attn_grouped")
            nc.scalar.copy(
                out=grouped[:].bitcast(F32).rearrange("p (g r u) -> p g r u", g=PASSES, u=2),
                in_=attn_t[:].rearrange("p (g u) r -> p g r u", u=2),
            )
            attn_grouped[j] = grouped

        def quantise_attn(j):
            codes = work.tile([P, PASSES * P], U32, align_bytes=64, name="attn_codes")
            scales = work.tile([P, PASSES * P], U8, align_bytes=64, name="attn_scales")
            nc.vector.quantize_mx(out=codes[:].bitcast(FP8X4), scales=scales[:], in_=attn_grouped[j][:])
            attn_mx[j] = (codes, scales)

        def add_bo_to_x(j):
            total = work.tile([P, D], F32, name="x_bo")
            nc.gpsimd.tensor_tensor(out=total[:], in0=x_sb[j][:], in1=bo_all[:], op=ALU.add)
            x_bo[j] = total

        def first_matmul(j):
            codes, scales = attn_mx[j]
            acc_1[j] = []
            for n in range(D // BANK):
                cols = slice(n * BANK, (n + 1) * BANK)
                acc = psum_1.tile([P, BANK], F32, name="acc_1")
                for g in range(PASSES):
                    toks = slice(g * P, (g + 1) * P)
                    nc.tensor.matmul_mx(
                        out=acc[:],
                        lhsT=codes[:, toks].bitcast(FP8X4),
                        lhsT_scale=scales[:, toks],
                        rhs=wo_codes[:, g, cols].bitcast(FP8X4),
                        rhs_scale=wo_scales[:, g, cols],
                        start=(g == 0),
                        stop=(g == PASSES - 1),
                    )
                acc_1[j].append(acc)

        def residual_and_rms(j):
            total = work.tile([P, D], F32, name="x_mid", bufs=3)
            for n in range(D // BANK):
                cols = slice(n * BANK, (n + 1) * BANK)
                nc.vector.tensor_tensor(out=total[:, cols], in0=acc_1[j][n][:], in1=x_bo[j][:, cols], op=ALU.add)
            nc.sync.dma_start(out=x_mid_rows[j * P : (j + 1) * P, :], in_=total[:])
            squares = work.tile([P, D], BF16)
            mean_sq = work.tile([P, 1], F32)
            nc.scalar.activation(out=squares[:], in_=total[:], func=ACT.Square, scale=D**-0.5, accum_out=mean_sq[:])
            mean_eps = work.tile([P, 1], F32)
            nc.gpsimd.tensor_scalar(out=mean_eps[:], in0=mean_sq[:], scalar1=EPS, scalar2=None, op0=ALU.add)
            power = work.tile([P, 1], F32, name="inv_rms")
            nc.gpsimd.tensor_tensor(out=power[:], in0=mean_eps[:], in1=minus_half[:], op=ALU.pow)
            x_mid[j] = total
            inv_rms[j] = power

        def normalise(j):
            normed = work.tile([P, D], BF16, name="h")
            nc.vector.scalar_tensor_tensor(
                out=normed[:], in0=x_mid[j][:], scalar=inv_rms[j][:, 0:1], in1=gain_all[:], op0=ALU.mult, op1=ALU.mult
            )
            h[j] = normed

        def transpose_h(j):
            h_t = psum_t.tile([P, PASSES * PACK, P], BF16)
            for w in range(PASSES * PACK):
                nc.tensor.transpose(h_t[:, w, :], h[j][:, w * P : (w + 1) * P], ident_bf16[:])
            grouped = work.tile([P, PASSES, P, PACK], BF16, align_bytes=64, name="h_grouped")
            nc.scalar.copy(out=grouped[:], in_=h_t[:].rearrange("p (g t) r -> p g r t", t=PACK))
            h_grouped[j] = grouped

        def quantise_h(j):
            codes = work.tile([P, PASSES * P], U32, align_bytes=64, name="h_codes")
            scales = work.tile([P, PASSES * P], U8, align_bytes=64, name="h_scales")
            nc.vector.quantize_mx(
                out=codes[:].bitcast(FP8X4), scales=scales[:], in_=h_grouped[j][:].rearrange("p g r t -> p (g r t)")
            )
            h_mx[j] = (codes, scales)

        def second_stage(j, q):
            codes, scales = h_mx[j]
            g_tile = result.tile([P, UNIT], F32)
            for n in range(UNIT // BANK):
                cols = slice(q * UNIT + n * BANK, q * UNIT + (n + 1) * BANK)
                acc = psum_2.tile([P, BANK], F32, name="acc_2")
                for g in range(PASSES):
                    toks = slice(g * P, (g + 1) * P)
                    nc.tensor.matmul_mx(
                        out=acc[:],
                        lhsT=codes[:, toks].bitcast(FP8X4),
                        lhsT_scale=scales[:, toks],
                        rhs=w1_codes[:, g, cols].bitcast(FP8X4),
                        rhs_scale=w1_scales[:, g, cols],
                        start=(g == 0),
                        stop=(g == PASSES - 1),
                    )
                nc.vector.tensor_tensor(
                    out=g_tile[:, n * BANK : (n + 1) * BANK], in0=acc[:], in1=b1_all[:, cols], op=ALU.add
                )
            nc.scalar.activation(out=g_tile[:], in_=g_tile[:], func=ACT.Gelu)
            nc.sync.dma_start(out=g_rows[j * P : (j + 1) * P, q * UNIT : (q + 1) * UNIT], in_=g_tile[:])

        def live(j):
            return 0 <= j < TOKEN_TILES

        steps_a_round = (WEIGHT_UNITS + 1 + LAG - 1) // LAG
        for i in range(-LAG, TOKEN_TILES):
            if live(i + 3):
                transpose_attn(i + 3)
            if live(i + 1):
                transpose_h(i + 1)
            if live(i + 2):
                residual_and_rms(i + 2)
            if live(i + 3):
                add_bo_to_x(i + 3)
                quantise_attn(i + 3)
            if live(i + 1):
                quantise_h(i + 1)
            if i < 0:
                first_step = (i + LAG) * steps_a_round
                for s in range(first_step, min(first_step + steps_a_round, WEIGHT_UNITS + 1)):
                    weight_step(s)
            else:
                for q in range(QUARTERS - 1):
                    second_stage(i, q)
            if live(i + 2):
                normalise(i + 2)
            if i >= 0:
                second_stage(i, QUARTERS - 1)
            if live(i + 3):
                first_matmul(i + 3)
